import numpy as np
import ml_dtypes


def mxq(x, axis, fmt="e4m3"):
    dtype, down = {"e4m3": (ml_dtypes.float8_e4m3fn, 7), "e5m2": (ml_dtypes.float8_e5m2, 14)}[fmt]
    v = np.moveaxis(np.asarray(x, np.float32).astype(ml_dtypes.bfloat16).astype(np.float64), axis, -1)
    blocks = v.reshape(v.shape[:-1] + (-1, 32))
    amax = np.abs(blocks).max(-1, keepdims=True)
    byte = np.maximum(np.where(amax > 0, np.frexp(amax)[1] - 1 + 127, 0) - down, 1)
    scale = np.exp2(byte - 127.0)
    codes = (blocks / scale).astype(np.float32).astype(dtype).astype(np.float64)
    return np.moveaxis((codes * scale).reshape(v.shape), -1, axis)


WIDE = False


def mx_kscale(k):
    if not WIDE:
        return np.ones(k)
    levels = np.array([10, -10, 5, -5, 0])
    a = np.random.permutation(np.resize(levels, k // 512 * 4)).reshape(k // 512, 4)
    idx = np.arange(k)
    return np.exp2(a[idx // 512, idx % 128 // 32])


BF16 = ml_dtypes.bfloat16


def bf(x):
    return np.asarray(x, np.float32).astype(BF16)


def f64(x):
    return np.asarray(x).astype(np.float64)


E2M1 = np.array([0.0, 0.5, 1.0, 1.5, 2.0, 3.0, 4.0, 6.0, -0.0, -0.5, -1.0, -1.5, -2.0, -3.0, -4.0, -6.0])


def pack_weight(w, fmt):
    k, n = w.shape
    w = f64(bf(w)).reshape(k // 32, 32, n)
    amax = np.abs(w).max(1)
    if fmt == "e4m3":
        byte = np.frexp(amax)[1] - 1 + 127 - 7
    else:
        mant, ex = np.frexp(amax / 6.0)
        byte = np.where(mant > 0.5, ex, ex - 1) + 127
    byte = np.clip(np.where(amax > 0, byte, 1), 1, 254)
    scaled = (w * np.exp2(127.0 - byte)[:, None, :]).reshape(k, n).astype(np.float32)
    by_word = np.ascontiguousarray(scaled.reshape(k // 512, 128, 4, n).transpose(0, 1, 3, 2))
    if fmt == "e4m3":
        words = by_word.astype(ml_dtypes.float8_e4m3fn).view(np.uint8)
    else:
        c = by_word.astype(ml_dtypes.float4_e2m1fn).view(np.uint8) & 0xF
        words = c[..., 0::2] | (c[..., 1::2] << 4)
    return np.ascontiguousarray(words), np.ascontiguousarray(byte.astype(np.uint8).reshape(k // 512, 16, n))


def unpack_weight(words, scales, fmt):
    g, p, n, _ = words.shape
    if fmt == "e4m3":
        vals = np.ascontiguousarray(words).view(ml_dtypes.float8_e4m3fn).astype(np.float64)
    else:
        nib = np.empty((g, p, n, 4), np.uint8)
        nib[..., 0::2] = words & 0xF
        nib[..., 1::2] = words >> 4
        vals = E2M1[nib]
    vals = vals * np.repeat(np.exp2(scales.astype(np.float64) - 127.0), 8, axis=1)[..., None]
    return vals.transpose(0, 1, 3, 2).reshape(g * 512, n)


B, D, DO, H, T, P = 8192, 512, 1024, 256, 8, 2


def setup_inputs():
    s = mx_kscale(D)
    transformed = bf(np.random.standard_normal((B, D)) * 1.2 * s)
    coeff = bf(np.random.standard_normal((B, P)) * 0.45)
    stack = np.random.standard_normal((P, D, D)) / np.sqrt(D) / s[None, :, None] * s[None, None, :]
    words, scales = pack_weight(stack.reshape(-1, D), "e4m3")
    return {"transformed": transformed,
            "coeff": coeff,
            "task_mats_words": words,
            "task_mats_scales": scales}


def reference(transformed, coeff, task_mats_words, task_mats_scales):
    x, c = f64(transformed), f64(coeff)
    m = unpack_weight(task_mats_words, task_mats_scales, "e4m3").reshape(P, D, D)
    for j in range(P):
        x = x + c[:, j:j + 1] * (mxq(x, 1, "e4m3") @ m[j])
    return x

@@ -1,0 +1,169 @@
+import concourse.mybir as mybir
+from concourse.masks import make_identity
+
+F32 = mybir.dt.float32
+BF16 = mybir.dt.bfloat16
+I32 = mybir.dt.int32
+U32 = mybir.dt.uint32
+U8 = mybir.dt.uint8
+FP8X4 = mybir.dt.float8_e4m3fn_x4
+MULT = mybir.AluOpType.mult
+ADD = mybir.AluOpType.add
+
+P = 128
+PACK = 4
+SAMPLES = 8192
+D = 512
+STEPS = 2
+TILES = SAMPLES // P
+PAIR = 2
+PAIRS = TILES // PAIR
+LOAD_TILES = 4
+QUADRANTS = 4
+
+FLOPS = 2 * STEPS * SAMPLES * D * D
+
+
+def tile_precomputedmetanet_pa_t_e_kernel(
+    tc, transformed, coeff, task_mats_words, task_mats_scales, out
+):
+    nc = tc.nc
+    x_dram = transformed.rearrange("(p j) d -> p j d", j=TILES)
+    out_dram = out.rearrange("(p j) d -> p j d", j=TILES)
+
+    with tc.tile_pool(name="keep", bufs=1) as keep, tc.tile_pool(
+        name="short", bufs=3
+    ) as short, tc.tile_pool(name="long", bufs=4) as long_lived, tc.psum_pool(
+        name="banks", bufs=2
+    ) as banks, tc.manual_schedule():
+        w_scales = keep.tile([P, STEPS, D], U8, align_bytes=64)
+        nc.vector.memset(w_scales[:].bitcast(I32), 0)
+        identity = keep.tile([P, P], F32)
+        make_identity(nc, identity[:])
+
+        x_loads = []
+        for c in range(TILES // LOAD_TILES):
+            x_loads.append(keep.tile([P, LOAD_TILES, D], BF16, name="x_load%d" % c))
+
+        def load_x(c):
+            nc.sync.dma_start(
+                out=x_loads[c][:], in_=x_dram[:, c * LOAD_TILES : (c + 1) * LOAD_TILES, :]
+            )
+
+        load_x(0)
+        for quadrant in range(QUADRANTS):
+            nc.sync.dma_start(
+                out=w_scales[32 * quadrant : 32 * quadrant + 4, :, :].bitcast(I32),
+                in_=task_mats_scales[:, 4 * quadrant : 4 * quadrant + 4, :]
+                .bitcast(I32)
+                .rearrange("s r n -> r s n"),
+            )
+        w_words = keep.tile([P, STEPS, D], U32, align_bytes=64)
+        nc.sync.dma_start(
+            out=w_words[:].bitcast(I32),
+            in_=task_mats_words.rearrange("s p n t -> p s (n t)").bitcast(I32),
+        )
+        coeff_bf16 = keep.tile([P, TILES, STEPS], BF16)
+        nc.sync.dma_start(out=coeff_bf16[:], in_=coeff.rearrange("(p j) s -> p j s", j=TILES))
+        for c in range(1, TILES // LOAD_TILES):
+            load_x(c)
+        coeff_f32 = keep.tile([P, TILES, STEPS], F32)
+        nc.vector.tensor_copy(out=coeff_f32[:], in_=coeff_bf16[:])
+
+        def x_tile(j):
+            return x_loads[j // LOAD_TILES][:, j % LOAD_TILES, :]
+
+        x_grouped, x_codes, x_scales, x1_kept = {}, {}, {}, {}
+        x1_grouped, x1_codes, x1_scales, products2 = {}, {}, {}, {}
+
+        def transpose_x(g):
+            x_t = banks.tile([P, PAIR, 2, P], F32)
+            for i in range(PAIR):
+                words = x_tile(PAIR * g + i).bitcast(F32)
+                for u in range(2):
+                    nc.tensor.transpose(x_t[:, i, u, :], words[:, u : D // 2 : 2], identity[:])
+            x_grouped[g] = short.tile([P, PAIR, P, PACK], BF16, align_bytes=64, name="x_grouped")
+            nc.scalar.copy(
+                out=x_grouped[g][:].bitcast(F32), in_=x_t[:].rearrange("p i u r -> p i r u")
+            )
+
+        def quantise(grouped, codes_of, scales_of, g, name):
+            codes_of[g] = short.tile([P, PAIR, P], U32, align_bytes=64, name=name + "_codes")
+            scales_of[g] = short.tile([P, PAIR, P], U8, align_bytes=64, name=name + "_scales")
+            nc.vector.quantize_mx(
+                out=codes_of[g][:].rearrange("p i r -> p (i r)").bitcast(FP8X4),
+                scales=scales_of[g][:].rearrange("p i r -> p (i r)"),
+                in_=grouped[g][:].rearrange("p i r t -> p (i r t)"),
+            )
+
+        def multiply(codes, scales, i, step):
+            product = banks.tile([P, D], F32, name="product%d" % step)
+            nc.tensor.matmul_mx(
+                out=product[:],
+                lhsT=codes[:, i, :].bitcast(FP8X4),
+                lhsT_scale=scales[:, i, :],
+                rhs=w_words[:, step, :].bitcast(FP8X4),
+                rhs_scale=w_scales[:, step, :],
+                start=True,
+                stop=True,
+            )
+            return product
+
+        def step1(g):
+            products = [multiply(x_codes[g], x_scales[g], i, 0) for i in range(PAIR)]
+            x1_kept[g] = long_lived.tile([P, PAIR, PACK, P], F32, name="x1_kept")
+            for i in range(PAIR):
+                j = PAIR * g + i
+                nc.vector.scalar_tensor_tensor(
+                    out=x1_kept[g][:, i, :, :],
+                    in0=products[i][:].rearrange("p (q t) -> p t q", t=PACK),
+                    scalar=coeff_f32[:, j, 0:1],
+                    in1=x_tile(j).rearrange("p (q t) -> p t q", t=PACK),
+                    op0=MULT,
+                    op1=ADD,
+                )
+
+        def transpose_x1(g):
+            x1_grouped[g] = short.tile([P, PAIR, P, PACK], BF16, align_bytes=64, name="x1_grouped")
+            for i in range(PAIR):
+                x1_t = banks.tile([P, PACK, P], F32)
+                for t in range(PACK):
+                    nc.tensor.transpose(x1_t[:, t, :], x1_kept[g][:, i, t, :], identity[:])
+                nc.scalar.copy(
+                    out=x1_grouped[g][:, i, :, :], in_=x1_t[:].rearrange("p t r -> p r t")
+                )
+
+        def step2(g):
+            products2[g] = [multiply(x1_codes[g], x1_scales[g], i, 1) for i in range(PAIR)]
+
+        def finish(g):
+            result = short.tile([P, PAIR, D], F32)
+            for i in range(PAIR):
+                nc.vector.scalar_tensor_tensor(
+                    out=result[:, i, :].rearrange("p (q t) -> p q t", t=PACK),
+                    in0=products2[g][i][:].rearrange("p (q t) -> p q t", t=PACK),
+                    scalar=coeff_f32[:, PAIR * g + i, 1:2],
+                    in1=x1_kept[g][:, i, :, :].rearrange("p t q -> p q t"),
+                    op0=MULT,
+                    op1=ADD,
+                )
+            nc.sync.dma_start(out=out_dram[:, PAIR * g : PAIR * (g + 1), :], in_=result[:])
+
+        def live(g):
+            return 0 <= g < PAIRS
+
+        for r in range(PAIRS + 4):
+            if live(r - 4):
+                finish(r - 4)
+            if live(r):
+                transpose_x(r)
+            if live(r - 2):
+                transpose_x1(r - 2)
+            if live(r):
+                quantise(x_grouped, x_codes, x_scales, r, "x")
+            if live(r - 1):
+                step1(r - 1)
+            if live(r - 2):
+                quantise(x1_grouped, x1_codes, x1_scales, r - 2, "x1")
+            if live(r - 3):
+                step2(r - 3)

@@ -111,14 +111,14 @@ def tile_precomputedmetanet_pa_t_e_kernel(
 
         def step1(g):
             products = [multiply(x_codes[g], x_scales[g], i, 0) for i in range(PAIR)]
-            x1_kept[g] = long_lived.tile([P, PAIR, PACK, P], F32, name="x1_kept")
+            x1_kept[g] = long_lived.tile([P, PAIR, D], F32, name="x1_kept")
             for i in range(PAIR):
                 j = PAIR * g + i
                 nc.vector.scalar_tensor_tensor(
-                    out=x1_kept[g][:, i, :, :],
-                    in0=products[i][:].rearrange("p (q t) -> p t q", t=PACK),
+                    out=x1_kept[g][:, i, :],
+                    in0=products[i][:],
                     scalar=coeff_f32[:, j, 0:1],
-                    in1=x_tile(j).rearrange("p (q t) -> p t q", t=PACK),
+                    in1=x_tile(j),
                     op0=MULT,
                     op1=ADD,
                 )
@@ -128,7 +128,7 @@ def tile_precomputedmetanet_pa_t_e_kernel(
             for i in range(PAIR):
                 x1_t = banks.tile([P, PACK, P], F32)
                 for t in range(PACK):
-                    nc.tensor.transpose(x1_t[:, t, :], x1_kept[g][:, i, t, :], identity[:])
+                    nc.tensor.transpose(x1_t[:, t, :], x1_kept[g][:, i, t:D:PACK], identity[:])
                 nc.scalar.copy(
                     out=x1_grouped[g][:, i, :, :], in_=x1_t[:].rearrange("p t r -> p r t")
                 )
@@ -140,10 +140,10 @@ def tile_precomputedmetanet_pa_t_e_kernel(
             result = short.tile([P, PAIR, D], F32)
             for i in range(PAIR):
                 nc.vector.scalar_tensor_tensor(
-                    out=result[:, i, :].rearrange("p (q t) -> p q t", t=PACK),
-                    in0=products2[g][i][:].rearrange("p (q t) -> p q t", t=PACK),
+                    out=result[:, i, :],
+                    in0=products2[g][i][:],
                     scalar=coeff_f32[:, PAIR * g + i, 1:2],
-                    in1=x1_kept[g][:, i, :, :].rearrange("p t q -> p q t"),
+                    in1=x1_kept[g][:, i, :],
                     op0=MULT,
                     op1=ADD,
                 )

@@ -9,6 +9,7 @@ U8 = mybir.dt.uint8
 FP8X4 = mybir.dt.float8_e4m3fn_x4
 MULT = mybir.AluOpType.mult
 ADD = mybir.AluOpType.add
+COPY = mybir.ActivationFunctionType.Copy
 
 P = 128
 PACK = 4
@@ -20,6 +21,7 @@ PAIR = 2
 PAIRS = TILES // PAIR
 LOAD_TILES = 4
 QUADRANTS = 4
+DEPTH = 6
 
 FLOPS = 2 * STEPS * SAMPLES * D * D
 
@@ -33,9 +35,9 @@ def tile_precomputedmetanet_pa_t_e_kernel(
 
     with tc.tile_pool(name="keep", bufs=1) as keep, tc.tile_pool(
         name="short", bufs=3
-    ) as short, tc.tile_pool(name="long", bufs=4) as long_lived, tc.psum_pool(
-        name="banks", bufs=2
-    ) as banks, tc.manual_schedule():
+    ) as short, tc.tile_pool(name="long", bufs=5) as long_lived, tc.psum_pool(
+        name="banks2", bufs=2
+    ) as banks2, tc.psum_pool(name="banks1", bufs=1) as banks1, tc.manual_schedule():
         w_scales = keep.tile([P, STEPS, D], U8, align_bytes=64)
         nc.vector.memset(w_scales[:].bitcast(I32), 0)
         identity = keep.tile([P, P], F32)
@@ -73,18 +75,20 @@ def tile_precomputedmetanet_pa_t_e_kernel(
         def x_tile(j):
             return x_loads[j // LOAD_TILES][:, j % LOAD_TILES, :]
 
-        x_grouped, x_codes, x_scales, x1_kept = {}, {}, {}, {}
-        x1_grouped, x1_codes, x1_scales, products2 = {}, {}, {}, {}
+        x_t, x_grouped, x_codes, x_scales, products1, x1_kept = {}, {}, {}, {}, {}, {}
+        x1_t, x1_grouped, x1_codes, x1_scales, products2, coeff_late, results = {}, {}, {}, {}, {}, {}, {}
 
         def transpose_x(g):
-            x_t = banks.tile([P, PAIR, 2, P], F32)
+            x_t[g] = banks2.tile([P, PAIR, 2, P], F32, name="x_t")
             for i in range(PAIR):
                 words = x_tile(PAIR * g + i).bitcast(F32)
                 for u in range(2):
-                    nc.tensor.transpose(x_t[:, i, u, :], words[:, u : D // 2 : 2], identity[:])
+                    nc.tensor.transpose(x_t[g][:, i, u, :], words[:, u : D // 2 : 2], identity[:])
+
+        def regroup_x(g):
             x_grouped[g] = short.tile([P, PAIR, P, PACK], BF16, align_bytes=64, name="x_grouped")
             nc.scalar.copy(
-                out=x_grouped[g][:].bitcast(F32), in_=x_t[:].rearrange("p i u r -> p i r u")
+                out=x_grouped[g][:].bitcast(F32), in_=x_t[g][:].rearrange("p i u r -> p i r u")
             )
 
         def quantise(grouped, codes_of, scales_of, g, name):
@@ -96,8 +100,7 @@ def tile_precomputedmetanet_pa_t_e_kernel(
                 in_=grouped[g][:].rearrange("p i r t -> p (i r t)"),
             )
 
-        def multiply(codes, scales, i, step):
-            product = banks.tile([P, D], F32, name="product%d" % step)
+        def multiply(product, codes, scales, i, step):
             nc.tensor.matmul_mx(
                 out=product[:],
                 lhsT=codes[:, i, :].bitcast(FP8X4),
@@ -107,16 +110,19 @@ def tile_precomputedmetanet_pa_t_e_kernel(
                 start=True,
                 stop=True,
             )
-            return product
 
-        def step1(g):
-            products = [multiply(x_codes[g], x_scales[g], i, 0) for i in range(PAIR)]
+        def multiply1(g):
+            products1[g] = [banks2.tile([P, D], F32, name="product1") for i in range(PAIR)]
+            for i in range(PAIR):
+                multiply(products1[g][i], x_codes[g], x_scales[g], i, 0)
+
+        def add1(g):
             x1_kept[g] = long_lived.tile([P, PAIR, D], F32, name="x1_kept")
             for i in range(PAIR):
                 j = PAIR * g + i
                 nc.vector.scalar_tensor_tensor(
                     out=x1_kept[g][:, i, :],
-                    in0=products[i][:],
+                    in0=products1[g][i][:],
                     scalar=coeff_f32[:, j, 0:1],
                     in1=x_tile(j),
                     op0=MULT,
@@ -124,46 +130,74 @@ def tile_precomputedmetanet_pa_t_e_kernel(
                 )
 
         def transpose_x1(g):
+            x1_t[g] = [banks2.tile([P, PACK, P], F32, name="x1_t") for i in range(PAIR)]
+            for i in range(PAIR):
+                for t in range(PACK):
+                    nc.tensor.transpose(
+                        x1_t[g][i][:, t, :], x1_kept[g][:, i, t:D:PACK], identity[:]
+                    )
+
+        def regroup_x1(g):
             x1_grouped[g] = short.tile([P, PAIR, P, PACK], BF16, align_bytes=64, name="x1_grouped")
             for i in range(PAIR):
-                x1_t = banks.tile([P, PACK, P], F32)
-                for t in range(PACK):
-                    nc.tensor.transpose(x1_t[:, t, :], x1_kept[g][:, i, t:D:PACK], identity[:])
                 nc.scalar.copy(
-                    out=x1_grouped[g][:, i, :, :], in_=x1_t[:].rearrange("p t r -> p r t")
+                    out=x1_grouped[g][:, i, :, :], in_=x1_t[g][i][:].rearrange("p t r -> p r t")
                 )
 
-        def step2(g):
-            products2[g] = [multiply(x1_codes[g], x1_scales[g], i, 1) for i in range(PAIR)]
-
-        def finish(g):
-            result = short.tile([P, PAIR, D], F32)
+        def multiply2(g):
+            products2[g] = [banks1.tile([P, D], F32, name="product2_%d" % i) for i in range(PAIR)]
             for i in range(PAIR):
-                nc.vector.scalar_tensor_tensor(
-                    out=result[:, i, :],
-                    in0=products2[g][i][:],
-                    scalar=coeff_f32[:, PAIR * g + i, 1:2],
-                    in1=x1_kept[g][:, i, :],
-                    op0=MULT,
-                    op1=ADD,
-                )
-            nc.sync.dma_start(out=out_dram[:, PAIR * g : PAIR * (g + 1), :], in_=result[:])
+                multiply(products2[g][i], x1_codes[g], x1_scales[g], i, 1)
+
+        def convert_coeff(g):
+            coeff_late[g] = short.tile([P, 1], F32, name="coeff_late")
+            nc.vector.tensor_copy(out=coeff_late[g][:], in_=coeff_bf16[:, PAIR * g, 1:2])
+
+        def finish_first_tile(g):
+            results[g] = short.tile([P, PAIR, D], F32, name="result")
+            scaled = short.tile([P, D], F32)
+            nc.scalar.activation(
+                out=scaled[:], in_=products2[g][0][:], func=COPY, scale=coeff_late[g][:, 0:1]
+            )
+            nc.gpsimd.tensor_tensor(
+                out=results[g][:, 0, :], in0=scaled[:], in1=x1_kept[g][:, 0, :], op=ADD
+            )
+
+        def finish_second_tile(g):
+            nc.vector.scalar_tensor_tensor(
+                out=results[g][:, 1, :],
+                in0=products2[g][1][:],
+                scalar=coeff_f32[:, PAIR * g + 1, 1:2],
+                in1=x1_kept[g][:, 1, :],
+                op0=MULT,
+                op1=ADD,
+            )
+            nc.sync.dma_start(out=out_dram[:, PAIR * g : PAIR * (g + 1), :], in_=results[g][:])
 
         def live(g):
             return 0 <= g < PAIRS
 
-        for r in range(PAIRS + 4):
+        for r in range(PAIRS + DEPTH):
+            if live(r - 3):
+                multiply1(r - 3)
+            if live(r - 6):
+                convert_coeff(r - 6)
+            if live(r - 5):
+                quantise(x1_grouped, x1_codes, x1_scales, r - 5, "x1")
+            if live(r - 2):
+                quantise(x_grouped, x_codes, x_scales, r - 2, "x")
+            if live(r - 6):
+                finish_first_tile(r - 6)
+                finish_second_tile(r - 6)
+            if live(r - 3):
+                add1(r - 3)
+            if live(r - 5):
+                multiply2(r - 5)
+            if live(r - 1):
+                regroup_x(r - 1)
             if live(r - 4):
-                finish(r - 4)
+                regroup_x1(r - 4)
             if live(r):
                 transpose_x(r)
-            if live(r - 2):
-                transpose_x1(r - 2)
-            if live(r):
-                quantise(x_grouped, x_codes, x_scales, r, "x")
-            if live(r - 1):
-                step1(r - 1)
-            if live(r - 2):
-                quantise(x1_grouped, x1_codes, x1_scales, r - 2, "x1")
             if live(r - 3):
-                step2(r - 3)
+                transpose_x1(r - 3)

@@ -21,7 +21,7 @@ PAIR = 2
 PAIRS = TILES // PAIR
 LOAD_TILES = 4
 QUADRANTS = 4
-DEPTH = 6
+DEPTH = 4
 
 FLOPS = 2 * STEPS * SAMPLES * D * D
 
@@ -117,14 +117,14 @@ def tile_precomputedmetanet_pa_t_e_kernel(
                 multiply(products1[g][i], x_codes[g], x_scales[g], i, 0)
 
         def add1(g):
-            x1_kept[g] = long_lived.tile([P, PAIR, D], F32, name="x1_kept")
+            x1_kept[g] = long_lived.tile([P, PAIR, PACK, P], F32, name="x1_kept")
             for i in range(PAIR):
                 j = PAIR * g + i
                 nc.vector.scalar_tensor_tensor(
-                    out=x1_kept[g][:, i, :],
-                    in0=products1[g][i][:],
+                    out=x1_kept[g][:, i, :, :],
+                    in0=products1[g][i][:].rearrange("p (q t) -> p t q", t=PACK),
                     scalar=coeff_f32[:, j, 0:1],
-                    in1=x_tile(j),
+                    in1=x_tile(j).rearrange("p (q t) -> p t q", t=PACK),
                     op0=MULT,
                     op1=ADD,
                 )
@@ -133,9 +133,7 @@ def tile_precomputedmetanet_pa_t_e_kernel(
             x1_t[g] = [banks2.tile([P, PACK, P], F32, name="x1_t") for i in range(PAIR)]
             for i in range(PAIR):
                 for t in range(PACK):
-                    nc.tensor.transpose(
-                        x1_t[g][i][:, t, :], x1_kept[g][:, i, t:D:PACK], identity[:]
-                    )
+                    nc.tensor.transpose(x1_t[g][i][:, t, :], x1_kept[g][:, i, t, :], identity[:])
 
         def regroup_x1(g):
             x1_grouped[g] = short.tile([P, PAIR, P, PACK], BF16, align_bytes=64, name="x1_grouped")
@@ -160,15 +158,18 @@ def tile_precomputedmetanet_pa_t_e_kernel(
                 out=scaled[:], in_=products2[g][0][:], func=COPY, scale=coeff_late[g][:, 0:1]
             )
             nc.gpsimd.tensor_tensor(
-                out=results[g][:, 0, :], in0=scaled[:], in1=x1_kept[g][:, 0, :], op=ADD
+                out=results[g][:, 0, :].rearrange("p (q t) -> p q t", t=PACK),
+                in0=scaled[:].rearrange("p (q t) -> p q t", t=PACK),
+                in1=x1_kept[g][:, 0, :, :].rearrange("p t q -> p q t"),
+                op=ADD,
             )
 
         def finish_second_tile(g):
             nc.vector.scalar_tensor_tensor(
-                out=results[g][:, 1, :],
-                in0=products2[g][1][:],
+                out=results[g][:, 1, :].rearrange("p (q t) -> p q t", t=PACK),
+                in0=products2[g][1][:].rearrange("p (q t) -> p q t", t=PACK),
                 scalar=coeff_f32[:, PAIR * g + 1, 1:2],
-                in1=x1_kept[g][:, 1, :],
+                in1=x1_kept[g][:, 1, :, :].rearrange("p t q -> p q t"),
                 op0=MULT,
                 op1=ADD,
             )
@@ -178,26 +179,22 @@ def tile_precomputedmetanet_pa_t_e_kernel(
             return 0 <= g < PAIRS
 
         for r in range(PAIRS + DEPTH):
-            if live(r - 3):
-                multiply1(r - 3)
-            if live(r - 6):
-                convert_coeff(r - 6)
-            if live(r - 5):
-                quantise(x1_grouped, x1_codes, x1_scales, r - 5, "x1")
             if live(r - 2):
-                quantise(x_grouped, x_codes, x_scales, r - 2, "x")
-            if live(r - 6):
-                finish_first_tile(r - 6)
-                finish_second_tile(r - 6)
-            if live(r - 3):
-                add1(r - 3)
-            if live(r - 5):
-                multiply2(r - 5)
-            if live(r - 1):
-                regroup_x(r - 1)
-            if live(r - 4):
-                regroup_x1(r - 4)
+                multiply1(r - 2)
+                add1(r - 2)
             if live(r):
                 transpose_x(r)
+                regroup_x(r)
+            if live(r - 4):
+                convert_coeff(r - 4)
             if live(r - 3):
-                transpose_x1(r - 3)
+                quantise(x1_grouped, x1_codes, x1_scales, r - 3, "x1")
+            if live(r - 1):
+                quantise(x_grouped, x_codes, x_scales, r - 1, "x")
+            if live(r - 4):
+                multiply2(r - 4)
+                finish_first_tile(r - 4)
+                finish_second_tile(r - 4)
+            if live(r - 2):
+                transpose_x1(r - 2)
+                regroup_x1(r - 2)

@@ -21,7 +21,7 @@ PAIR = 2
 PAIRS = TILES // PAIR
 LOAD_TILES = 4
 QUADRANTS = 4
-DEPTH = 4
+DEPTH = 6
 
 FLOPS = 2 * STEPS * SAMPLES * D * D
 
@@ -35,7 +35,7 @@ def tile_precomputedmetanet_pa_t_e_kernel(
 
     with tc.tile_pool(name="keep", bufs=1) as keep, tc.tile_pool(
         name="short", bufs=3
-    ) as short, tc.tile_pool(name="long", bufs=5) as long_lived, tc.psum_pool(
+    ) as short, tc.tile_pool(name="long", bufs=6) as long_lived, tc.psum_pool(
         name="banks2", bufs=2
     ) as banks2, tc.psum_pool(name="banks1", bufs=1) as banks1, tc.manual_schedule():
         w_scales = keep.tile([P, STEPS, D], U8, align_bytes=64)
@@ -179,22 +179,22 @@ def tile_precomputedmetanet_pa_t_e_kernel(
             return 0 <= g < PAIRS
 
         for r in range(PAIRS + DEPTH):
-            if live(r - 2):
-                multiply1(r - 2)
-                add1(r - 2)
+            if live(r - 3):
+                multiply1(r - 3)
+                add1(r - 3)
             if live(r):
                 transpose_x(r)
                 regroup_x(r)
-            if live(r - 4):
-                convert_coeff(r - 4)
-            if live(r - 3):
-                quantise(x1_grouped, x1_codes, x1_scales, r - 3, "x1")
+            if live(r - 6):
+                convert_coeff(r - 6)
+            if live(r - 5):
+                quantise(x1_grouped, x1_codes, x1_scales, r - 5, "x1")
             if live(r - 1):
                 quantise(x_grouped, x_codes, x_scales, r - 1, "x")
+            if live(r - 6):
+                multiply2(r - 6)
+                finish_first_tile(r - 6)
+                finish_second_tile(r - 6)
             if live(r - 4):
-                multiply2(r - 4)
-                finish_first_tile(r - 4)
-                finish_second_tile(r - 4)
-            if live(r - 2):
-                transpose_x1(r - 2)
-                regroup_x1(r - 2)
+                transpose_x1(r - 4)
+                regroup_x1(r - 4)

@@ -22,6 +22,8 @@ PAIRS = TILES // PAIR
 LOAD_TILES = 4
 QUADRANTS = 4
 DEPTH = 6
+X1 = 0
+X = 1
 
 FLOPS = 2 * STEPS * SAMPLES * D * D
 
@@ -35,7 +37,9 @@ def tile_precomputedmetanet_pa_t_e_kernel(
 
     with tc.tile_pool(name="keep", bufs=1) as keep, tc.tile_pool(
         name="short", bufs=3
-    ) as short, tc.tile_pool(name="long", bufs=6) as long_lived, tc.psum_pool(
+    ) as short, tc.tile_pool(name="long", bufs=6) as long_lived, tc.tile_pool(
+        name="quantised", bufs=4
+    ) as quantised, tc.psum_pool(
         name="banks2", bufs=2
     ) as banks2, tc.psum_pool(name="banks1", bufs=1) as banks1, tc.manual_schedule():
         w_scales = keep.tile([P, STEPS, D], U8, align_bytes=64)
@@ -72,11 +76,22 @@ def tile_precomputedmetanet_pa_t_e_kernel(
         coeff_f32 = keep.tile([P, TILES, STEPS], F32)
         nc.vector.tensor_copy(out=coeff_f32[:], in_=coeff_bf16[:])
 
+        def live(g):
+            return 0 <= g < PAIRS
+
         def x_tile(j):
             return x_loads[j // LOAD_TILES][:, j % LOAD_TILES, :]
 
-        x_t, x_grouped, x_codes, x_scales, products1, x1_kept = {}, {}, {}, {}, {}, {}
-        x1_t, x1_grouped, x1_codes, x1_scales, products2, coeff_late, results = {}, {}, {}, {}, {}, {}, {}
+        x_t, products1, x1_kept = {}, {}, {}
+        x1_t, products2, coeff_late, results = {}, {}, {}, {}
+        grouped, codes, scales = {}, {}, {}
+
+        def grouped_of(s):
+            if s not in grouped:
+                grouped[s] = short.tile(
+                    [P, 2, PAIR, P, PACK], BF16, align_bytes=64, name="grouped"
+                )
+            return grouped[s]
 
         def transpose_x(g):
             x_t[g] = banks2.tile([P, PAIR, 2, P], F32, name="x_t")
@@ -86,25 +101,31 @@ def tile_precomputedmetanet_pa_t_e_kernel(
                     nc.tensor.transpose(x_t[g][:, i, u, :], words[:, u : D // 2 : 2], identity[:])
 
         def regroup_x(g):
-            x_grouped[g] = short.tile([P, PAIR, P, PACK], BF16, align_bytes=64, name="x_grouped")
             nc.scalar.copy(
-                out=x_grouped[g][:].bitcast(F32), in_=x_t[g][:].rearrange("p i u r -> p i r u")
+                out=grouped_of(g)[:, X, :, :, :].bitcast(F32),
+                in_=x_t[g][:].rearrange("p i u r -> p i r u"),
             )
 
-        def quantise(grouped, codes_of, scales_of, g, name):
-            codes_of[g] = short.tile([P, PAIR, P], U32, align_bytes=64, name=name + "_codes")
-            scales_of[g] = short.tile([P, PAIR, P], U8, align_bytes=64, name=name + "_scales")
+        def quantise(s):
+            halves = [h for h in (X1, X) if live(s - 4 if h == X1 else s)]
+            first, count = halves[0], len(halves)
+            codes[s] = quantised.tile([P, 2, PAIR, P], U32, align_bytes=64, name="codes")
+            scales[s] = quantised.tile([P, 2, PAIR, P], U8, align_bytes=64, name="scales")
             nc.vector.quantize_mx(
-                out=codes_of[g][:].rearrange("p i r -> p (i r)").bitcast(FP8X4),
-                scales=scales_of[g][:].rearrange("p i r -> p (i r)"),
-                in_=grouped[g][:].rearrange("p i r t -> p (i r t)"),
+                out=codes[s][:, first : first + count, :, :]
+                .rearrange("p h i r -> p (h i r)")
+                .bitcast(FP8X4),
+                scales=scales[s][:, first : first + count, :, :].rearrange("p h i r -> p (h i r)"),
+                in_=grouped[s][:, first : first + count, :, :, :].rearrange(
+                    "p h i r t -> p (h i r t)"
+                ),
             )
 
-        def multiply(product, codes, scales, i, step):
+        def multiply(product, s, half, i, step):
             nc.tensor.matmul_mx(
                 out=product[:],
-                lhsT=codes[:, i, :].bitcast(FP8X4),
-                lhsT_scale=scales[:, i, :],
+                lhsT=codes[s][:, half, i, :].bitcast(FP8X4),
+                lhsT_scale=scales[s][:, half, i, :],
                 rhs=w_words[:, step, :].bitcast(FP8X4),
                 rhs_scale=w_scales[:, step, :],
                 start=True,
@@ -114,7 +135,7 @@ def tile_precomputedmetanet_pa_t_e_kernel(
         def multiply1(g):
             products1[g] = [banks2.tile([P, D], F32, name="product1") for i in range(PAIR)]
             for i in range(PAIR):
-                multiply(products1[g][i], x_codes[g], x_scales[g], i, 0)
+                multiply(products1[g][i], g, X, i, 0)
 
         def add1(g):
             x1_kept[g] = long_lived.tile([P, PAIR, PACK, P], F32, name="x1_kept")
@@ -136,16 +157,16 @@ def tile_precomputedmetanet_pa_t_e_kernel(
                     nc.tensor.transpose(x1_t[g][i][:, t, :], x1_kept[g][:, i, t, :], identity[:])
 
         def regroup_x1(g):
-            x1_grouped[g] = short.tile([P, PAIR, P, PACK], BF16, align_bytes=64, name="x1_grouped")
             for i in range(PAIR):
                 nc.scalar.copy(
-                    out=x1_grouped[g][:, i, :, :], in_=x1_t[g][i][:].rearrange("p t r -> p r t")
+                    out=grouped_of(g + 4)[:, X1, i, :, :],
+                    in_=x1_t[g][i][:].rearrange("p t r -> p r t"),
                 )
 
         def multiply2(g):
             products2[g] = [banks1.tile([P, D], F32, name="product2_%d" % i) for i in range(PAIR)]
             for i in range(PAIR):
-                multiply(products2[g][i], x1_codes[g], x1_scales[g], i, 1)
+                multiply(products2[g][i], g + 4, X1, i, 1)
 
         def convert_coeff(g):
             coeff_late[g] = short.tile([P, 1], F32, name="coeff_late")
@@ -175,9 +196,6 @@ def tile_precomputedmetanet_pa_t_e_kernel(
             )
             nc.sync.dma_start(out=out_dram[:, PAIR * g : PAIR * (g + 1), :], in_=results[g][:])
 
-        def live(g):
-            return 0 <= g < PAIRS
-
         for r in range(PAIRS + DEPTH):
             if live(r - 3):
                 multiply1(r - 3)
@@ -187,10 +205,8 @@ def tile_precomputedmetanet_pa_t_e_kernel(
                 regroup_x(r)
             if live(r - 6):
                 convert_coeff(r - 6)
-            if live(r - 5):
-                quantise(x1_grouped, x1_codes, x1_scales, r - 5, "x1")
-            if live(r - 1):
-                quantise(x_grouped, x_codes, x_scales, r - 1, "x")
+            if live(r - 5) or live(r - 1):
+                quantise(r - 1)
             if live(r - 6):
                 multiply2(r - 6)
                 finish_first_tile(r - 6)

@@ -21,7 +21,10 @@ PAIR = 2
 PAIRS = TILES // PAIR
 LOAD_TILES = 4
 QUADRANTS = 4
-DEPTH = 6
+LAG_M1 = 3
+LAG_ROUND = 4
+LAG_Y = 5
+LAG_M2 = 7
 X1 = 0
 X = 1
 
@@ -82,8 +85,11 @@ def tile_precomputedmetanet_pa_t_e_kernel(
         def x_tile(j):
             return x_loads[j // LOAD_TILES][:, j % LOAD_TILES, :]
 
-        x_t, products1, x1_kept = {}, {}, {}
-        x1_t, products2, coeff_late, results = {}, {}, {}, {}
+        ones = keep.tile([P, 1], F32)
+        nc.vector.memset(ones[:], 1.0)
+
+        x_t, products1, x1_kept, x1_rounded = {}, {}, {}, {}
+        x1_t, products2, results, gates = {}, {}, {}, {}
         grouped, codes, scales = {}, {}, {}
 
         def grouped_of(s):
@@ -100,14 +106,14 @@ def tile_precomputedmetanet_pa_t_e_kernel(
                 for u in range(2):
                     nc.tensor.transpose(x_t[g][:, i, u, :], words[:, u : D // 2 : 2], identity[:])
 
-        def regroup_x(g):
+        def regroup(transposed, s, half):
             nc.scalar.copy(
-                out=grouped_of(g)[:, X, :, :, :].bitcast(F32),
-                in_=x_t[g][:].rearrange("p i u r -> p i r u"),
+                out=grouped_of(s)[:, half, :, :, :].bitcast(F32),
+                in_=transposed[:].rearrange("p i u r -> p i r u"),
             )
 
         def quantise(s):
-            halves = [h for h in (X1, X) if live(s - 4 if h == X1 else s)]
+            halves = [h for h in (X1, X) if live(s - LAG_Y if h == X1 else s)]
             first, count = halves[0], len(halves)
             codes[s] = quantised.tile([P, 2, PAIR, P], U32, align_bytes=64, name="codes")
             scales[s] = quantised.tile([P, 2, PAIR, P], U8, align_bytes=64, name="scales")
@@ -138,79 +144,89 @@ def tile_precomputedmetanet_pa_t_e_kernel(
                 multiply(products1[g][i], g, X, i, 0)
 
         def add1(g):
-            x1_kept[g] = long_lived.tile([P, PAIR, PACK, P], F32, name="x1_kept")
+            x1_kept[g] = long_lived.tile([P, PAIR, D], F32, name="x1_kept")
             for i in range(PAIR):
                 j = PAIR * g + i
                 nc.vector.scalar_tensor_tensor(
-                    out=x1_kept[g][:, i, :, :],
-                    in0=products1[g][i][:].rearrange("p (q t) -> p t q", t=PACK),
+                    out=x1_kept[g][:, i, :],
+                    in0=products1[g][i][:],
                     scalar=coeff_f32[:, j, 0:1],
-                    in1=x_tile(j).rearrange("p (q t) -> p t q", t=PACK),
+                    in1=x_tile(j),
                     op0=MULT,
                     op1=ADD,
                 )
 
-        def transpose_x1(g):
-            x1_t[g] = [banks2.tile([P, PACK, P], F32, name="x1_t") for i in range(PAIR)]
-            for i in range(PAIR):
-                for t in range(PACK):
-                    nc.tensor.transpose(x1_t[g][i][:, t, :], x1_kept[g][:, i, t, :], identity[:])
+        def open_gate(g):
+            gates[g] = short.tile([P, 1], F32, name="gate")
+            nc.vector.tensor_copy(out=gates[g][:], in_=ones[:])
 
-        def regroup_x1(g):
+        def round_x1(g):
+            x1_rounded[g] = short.tile([P, PAIR, 2, P, 2], BF16, name="x1_rounded")
+            nc.gpsimd.tensor_scalar(
+                out=x1_rounded[g][:, 0, :, :, :],
+                in0=x1_kept[g][:, 0, :].rearrange("s (p u e) -> s u p e", u=2, e=2),
+                scalar1=gates[g][:, 0:1],
+                scalar2=0.0,
+                op0=MULT,
+                op1=ADD,
+            )
+            nc.scalar.copy(
+                out=x1_rounded[g][:, 1, :, :, :],
+                in_=x1_kept[g][:, 1, :].rearrange("s (p u e) -> s u p e", u=2, e=2),
+            )
+
+        def transpose_x1(g):
+            x1_t[g] = banks2.tile([P, PAIR, 2, P], F32, name="x1_t")
             for i in range(PAIR):
-                nc.scalar.copy(
-                    out=grouped_of(g + 4)[:, X1, i, :, :],
-                    in_=x1_t[g][i][:].rearrange("p t r -> p r t"),
-                )
+                words = x1_rounded[g][:, i, :, :, :].rearrange("s u p e -> s (u p e)").bitcast(F32)
+                for u in range(2):
+                    nc.tensor.transpose(
+                        x1_t[g][:, i, u, :], words[:, u * P : (u + 1) * P], identity[:]
+                    )
 
         def multiply2(g):
             products2[g] = [banks1.tile([P, D], F32, name="product2_%d" % i) for i in range(PAIR)]
             for i in range(PAIR):
-                multiply(products2[g][i], g + 4, X1, i, 1)
-
-        def convert_coeff(g):
-            coeff_late[g] = short.tile([P, 1], F32, name="coeff_late")
-            nc.vector.tensor_copy(out=coeff_late[g][:], in_=coeff_bf16[:, PAIR * g, 1:2])
+                multiply(products2[g][i], g + LAG_Y, X1, i, 1)
 
         def finish_first_tile(g):
             results[g] = short.tile([P, PAIR, D], F32, name="result")
             scaled = short.tile([P, D], F32)
             nc.scalar.activation(
-                out=scaled[:], in_=products2[g][0][:], func=COPY, scale=coeff_late[g][:, 0:1]
+                out=scaled[:], in_=products2[g][0][:], func=COPY, scale=coeff_f32[:, PAIR * g, 1:2]
             )
             nc.gpsimd.tensor_tensor(
-                out=results[g][:, 0, :].rearrange("p (q t) -> p q t", t=PACK),
-                in0=scaled[:].rearrange("p (q t) -> p q t", t=PACK),
-                in1=x1_kept[g][:, 0, :, :].rearrange("p t q -> p q t"),
-                op=ADD,
+                out=results[g][:, 0, :], in0=scaled[:], in1=x1_kept[g][:, 0, :], op=ADD
             )
 
         def finish_second_tile(g):
             nc.vector.scalar_tensor_tensor(
-                out=results[g][:, 1, :].rearrange("p (q t) -> p q t", t=PACK),
-                in0=products2[g][1][:].rearrange("p (q t) -> p q t", t=PACK),
+                out=results[g][:, 1, :],
+                in0=products2[g][1][:],
                 scalar=coeff_f32[:, PAIR * g + 1, 1:2],
-                in1=x1_kept[g][:, 1, :, :].rearrange("p t q -> p q t"),
+                in1=x1_kept[g][:, 1, :],
                 op0=MULT,
                 op1=ADD,
             )
             nc.sync.dma_start(out=out_dram[:, PAIR * g : PAIR * (g + 1), :], in_=results[g][:])
 
-        for r in range(PAIRS + DEPTH):
-            if live(r - 3):
-                multiply1(r - 3)
-                add1(r - 3)
+        for r in range(PAIRS + LAG_M2):
+            if live(r - LAG_M1):
+                multiply1(r - LAG_M1)
+                add1(r - LAG_M1)
             if live(r):
                 transpose_x(r)
-                regroup_x(r)
-            if live(r - 6):
-                convert_coeff(r - 6)
-            if live(r - 5) or live(r - 1):
+                regroup(x_t[r], r, X)
+            if live(r - LAG_ROUND):
+                open_gate(r - LAG_ROUND)
+            if live(r - 1 - LAG_Y) or live(r - 1):
                 quantise(r - 1)
-            if live(r - 6):
-                multiply2(r - 6)
-                finish_first_tile(r - 6)
-                finish_second_tile(r - 6)
-            if live(r - 4):
-                transpose_x1(r - 4)
-                regroup_x1(r - 4)
+            if live(r - LAG_ROUND):
+                round_x1(r - LAG_ROUND)
+            if live(r - LAG_M2):
+                multiply2(r - LAG_M2)
+                finish_first_tile(r - LAG_M2)
+                finish_second_tile(r - LAG_M2)
+            if live(r - LAG_Y):
+                transpose_x1(r - LAG_Y)
+                regroup(x1_t[r - LAG_Y], r, X1)

@@ -22,9 +22,8 @@ PAIRS = TILES // PAIR
 LOAD_TILES = 4
 QUADRANTS = 4
 LAG_M1 = 3
-LAG_ROUND = 4
-LAG_Y = 5
-LAG_M2 = 7
+LAG_Y = 4
+LAG_M2 = 6
 X1 = 0
 X = 1
 
@@ -85,11 +84,8 @@ def tile_precomputedmetanet_pa_t_e_kernel(
         def x_tile(j):
             return x_loads[j // LOAD_TILES][:, j % LOAD_TILES, :]
 
-        ones = keep.tile([P, 1], F32)
-        nc.vector.memset(ones[:], 1.0)
-
         x_t, products1, x1_kept, x1_rounded = {}, {}, {}, {}
-        x1_t, products2, results, gates = {}, {}, {}, {}
+        x1_t, products2, results = {}, {}, {}
         grouped, codes, scales = {}, {}, {}
 
         def grouped_of(s):
@@ -143,37 +139,35 @@ def tile_precomputedmetanet_pa_t_e_kernel(
             for i in range(PAIR):
                 multiply(products1[g][i], g, X, i, 0)
 
-        def add1(g):
-            x1_kept[g] = long_lived.tile([P, PAIR, D], F32, name="x1_kept")
-            for i in range(PAIR):
-                j = PAIR * g + i
-                nc.vector.scalar_tensor_tensor(
-                    out=x1_kept[g][:, i, :],
-                    in0=products1[g][i][:],
-                    scalar=coeff_f32[:, j, 0:1],
-                    in1=x_tile(j),
-                    op0=MULT,
-                    op1=ADD,
-                )
-
-        def open_gate(g):
-            gates[g] = short.tile([P, 1], F32, name="gate")
-            nc.vector.tensor_copy(out=gates[g][:], in_=ones[:])
-
-        def round_x1(g):
-            x1_rounded[g] = short.tile([P, PAIR, 2, P, 2], BF16, name="x1_rounded")
-            nc.gpsimd.tensor_scalar(
-                out=x1_rounded[g][:, 0, :, :, :],
-                in0=x1_kept[g][:, 0, :].rearrange("s (p u e) -> s u p e", u=2, e=2),
-                scalar1=gates[g][:, 0:1],
-                scalar2=0.0,
+        def add1(g, i):
+            if i == 0:
+                x1_kept[g] = long_lived.tile([P, PAIR, D], F32, name="x1_kept")
+            j = PAIR * g + i
+            nc.vector.scalar_tensor_tensor(
+                out=x1_kept[g][:, i, :],
+                in0=products1[g][i][:],
+                scalar=coeff_f32[:, j, 0:1],
+                in1=x_tile(j),
                 op0=MULT,
                 op1=ADD,
             )
-            nc.scalar.copy(
-                out=x1_rounded[g][:, 1, :, :, :],
-                in_=x1_kept[g][:, 1, :].rearrange("s (p u e) -> s u p e", u=2, e=2),
-            )
+
+        def round_x1(g, i):
+            if i == 0:
+                x1_rounded[g] = short.tile([P, PAIR, 2, P, 2], BF16, name="x1_rounded")
+                nc.gpsimd.tensor_scalar(
+                    out=x1_rounded[g][:, 0, :, :, :],
+                    in0=x1_kept[g][:, 0, :].rearrange("s (p u e) -> s u p e", u=2, e=2),
+                    scalar1=1.0,
+                    scalar2=0.0,
+                    op0=MULT,
+                    op1=ADD,
+                )
+            else:
+                nc.scalar.copy(
+                    out=x1_rounded[g][:, 1, :, :, :],
+                    in_=x1_kept[g][:, 1, :].rearrange("s (p u e) -> s u p e", u=2, e=2),
+                )
 
         def transpose_x1(g):
             x1_t[g] = banks2.tile([P, PAIR, 2, P], F32, name="x1_t")
@@ -213,16 +207,15 @@ def tile_precomputedmetanet_pa_t_e_kernel(
         for r in range(PAIRS + LAG_M2):
             if live(r - LAG_M1):
                 multiply1(r - LAG_M1)
-                add1(r - LAG_M1)
+                add1(r - LAG_M1, 0)
+            if live(r - 1 - LAG_Y) or live(r - 1):
+                quantise(r - 1)
+            if live(r - LAG_M1):
+                add1(r - LAG_M1, 1)
+                round_x1(r - LAG_M1, 0)
             if live(r):
                 transpose_x(r)
                 regroup(x_t[r], r, X)
-            if live(r - LAG_ROUND):
-                open_gate(r - LAG_ROUND)
-            if live(r - 1 - LAG_Y) or live(r - 1):
-                quantise(r - 1)
-            if live(r - LAG_ROUND):
-                round_x1(r - LAG_ROUND)
             if live(r - LAG_M2):
                 multiply2(r - LAG_M2)
                 finish_first_tile(r - LAG_M2)
@@ -230,3 +223,5 @@ def tile_precomputedmetanet_pa_t_e_kernel(
             if live(r - LAG_Y):
                 transpose_x1(r - LAG_Y)
                 regroup(x1_t[r - LAG_Y], r, X1)
+            if live(r - LAG_M1):
+                round_x1(r - LAG_M1, 1)

@@ -20,10 +20,12 @@ TILES = SAMPLES // P
 PAIR = 2
 PAIRS = TILES // PAIR
 LOAD_TILES = 4
+LOADS_AHEAD = 2
 QUADRANTS = 4
 LAG_M1 = 3
 LAG_Y = 4
 LAG_M2 = 6
+HEAD_LOADS = PAIR * (LAG_M1 + 1) // LOAD_TILES
 X1 = 0
 X = 1
 
@@ -41,7 +43,7 @@ def tile_precomputedmetanet_pa_t_e_kernel(
         name="short", bufs=3
     ) as short, tc.tile_pool(name="long", bufs=6) as long_lived, tc.tile_pool(
         name="quantised", bufs=4
-    ) as quantised, tc.psum_pool(
+    ) as quantised, tc.tile_pool(name="stored", bufs=6) as stored, tc.psum_pool(
         name="banks2", bufs=2
     ) as banks2, tc.psum_pool(name="banks1", bufs=1) as banks1, tc.manual_schedule():
         w_scales = keep.tile([P, STEPS, D], U8, align_bytes=64)
@@ -53,12 +55,22 @@ def tile_precomputedmetanet_pa_t_e_kernel(
         for c in range(TILES // LOAD_TILES):
             x_loads.append(keep.tile([P, LOAD_TILES, D], BF16, name="x_load%d" % c))
 
-        def load_x(c):
+        def load_x(first, count):
+            c, at = first // LOAD_TILES, first % LOAD_TILES
             nc.sync.dma_start(
-                out=x_loads[c][:], in_=x_dram[:, c * LOAD_TILES : (c + 1) * LOAD_TILES, :]
+                out=x_loads[c][:, at : at + count, :], in_=x_dram[:, first : first + count, :]
             )
 
-        load_x(0)
+        w_words = keep.tile([P, STEPS, D], U32, align_bytes=64)
+
+        def load_words(step):
+            nc.sync.dma_start(
+                out=w_words[:, step, :].bitcast(I32),
+                in_=task_mats_words[step].rearrange("p n t -> p (n t)").bitcast(I32),
+            )
+
+        for g in range(LAG_M1):
+            load_x(PAIR * g, PAIR)
         for quadrant in range(QUADRANTS):
             nc.sync.dma_start(
                 out=w_scales[32 * quadrant : 32 * quadrant + 4, :, :].bitcast(I32),
@@ -66,17 +78,15 @@ def tile_precomputedmetanet_pa_t_e_kernel(
                 .bitcast(I32)
                 .rearrange("s r n -> r s n"),
             )
-        w_words = keep.tile([P, STEPS, D], U32, align_bytes=64)
-        nc.sync.dma_start(
-            out=w_words[:].bitcast(I32),
-            in_=task_mats_words.rearrange("s p n t -> p s (n t)").bitcast(I32),
-        )
+        load_words(0)
         coeff_bf16 = keep.tile([P, TILES, STEPS], BF16)
         nc.sync.dma_start(out=coeff_bf16[:], in_=coeff.rearrange("(p j) s -> p j s", j=TILES))
-        for c in range(1, TILES // LOAD_TILES):
-            load_x(c)
+        load_x(PAIR * LAG_M1, PAIR)
+        load_words(1)
+        for c in range(HEAD_LOADS, HEAD_LOADS + LOADS_AHEAD):
+            load_x(c * LOAD_TILES, LOAD_TILES)
         coeff_f32 = keep.tile([P, TILES, STEPS], F32)
-        nc.vector.tensor_copy(out=coeff_f32[:], in_=coeff_bf16[:])
+        nc.gpsimd.tensor_copy(out=coeff_f32[:], in_=coeff_bf16[:])
 
         def live(g):
             return 0 <= g < PAIRS
@@ -146,7 +156,7 @@ def tile_precomputedmetanet_pa_t_e_kernel(
             nc.vector.scalar_tensor_tensor(
                 out=x1_kept[g][:, i, :],
                 in0=products1[g][i][:],
-                scalar=coeff_f32[:, j, 0:1],
+                scalar=coeff_bf16[:, j, 0:1],
                 in1=x_tile(j),
                 op0=MULT,
                 op1=ADD,
@@ -183,28 +193,50 @@ def tile_precomputedmetanet_pa_t_e_kernel(
             for i in range(PAIR):
                 multiply(products2[g][i], g + LAG_Y, X1, i, 1)
 
-        def finish_first_tile(g):
-            results[g] = short.tile([P, PAIR, D], F32, name="result")
+        def finish_by_scalar_and_gpsimd(g, i):
             scaled = short.tile([P, D], F32)
             nc.scalar.activation(
-                out=scaled[:], in_=products2[g][0][:], func=COPY, scale=coeff_f32[:, PAIR * g, 1:2]
+                out=scaled[:],
+                in_=products2[g][i][:],
+                func=COPY,
+                scale=coeff_f32[:, PAIR * g + i, 1:2],
             )
             nc.gpsimd.tensor_tensor(
-                out=results[g][:, 0, :], in0=scaled[:], in1=x1_kept[g][:, 0, :], op=ADD
+                out=results[g][:, i, :], in0=scaled[:], in1=x1_kept[g][:, i, :], op=ADD
             )
 
-        def finish_second_tile(g):
+        def finish_by_vector(g, i):
             nc.vector.scalar_tensor_tensor(
-                out=results[g][:, 1, :],
-                in0=products2[g][1][:],
-                scalar=coeff_f32[:, PAIR * g + 1, 1:2],
-                in1=x1_kept[g][:, 1, :],
+                out=results[g][:, i, :],
+                in0=products2[g][i][:],
+                scalar=coeff_bf16[:, PAIR * g + i, 1:2],
+                in1=x1_kept[g][:, i, :],
                 op0=MULT,
                 op1=ADD,
             )
-            nc.sync.dma_start(out=out_dram[:, PAIR * g : PAIR * (g + 1), :], in_=results[g][:])
+
+        def store(g, first, count):
+            j = PAIR * g + first
+            nc.sync.dma_start(
+                out=out_dram[:, j : j + count, :], in_=results[g][:, first : first + count, :]
+            )
+
+        def finish(g):
+            results[g] = stored.tile([P, PAIR, D], F32, name="result")
+            if g + LAG_M2 < PAIRS + LAG_M1:
+                finish_by_scalar_and_gpsimd(g, 0)
+                finish_by_vector(g, 1)
+                store(g, 0, PAIR)
+            else:
+                for i in range(PAIR):
+                    finish_by_vector(g, i)
+                    store(g, i, 1)
 
         for r in range(PAIRS + LAG_M2):
+            if r % (LOAD_TILES // PAIR) == 0:
+                c = r * PAIR // LOAD_TILES + HEAD_LOADS + LOADS_AHEAD
+                if c < TILES // LOAD_TILES:
+                    load_x(c * LOAD_TILES, LOAD_TILES)
             if live(r - LAG_M1):
                 multiply1(r - LAG_M1)
                 add1(r - LAG_M1, 0)
@@ -218,8 +250,7 @@ def tile_precomputedmetanet_pa_t_e_kernel(
                 regroup(x_t[r], r, X)
             if live(r - LAG_M2):
                 multiply2(r - LAG_M2)
-                finish_first_tile(r - LAG_M2)
-                finish_second_tile(r - LAG_M2)
+                finish(r - LAG_M2)
             if live(r - LAG_Y):
                 transpose_x1(r - LAG_Y)
                 regroup(x1_t[r - LAG_Y], r, X1)

@@ -245,12 +245,12 @@ def tile_precomputedmetanet_pa_t_e_kernel(
             if live(r - LAG_M1):
                 add1(r - LAG_M1, 1)
                 round_x1(r - LAG_M1, 0)
-            if live(r):
-                transpose_x(r)
-                regroup(x_t[r], r, X)
             if live(r - LAG_M2):
                 multiply2(r - LAG_M2)
                 finish(r - LAG_M2)
+            if live(r):
+                transpose_x(r)
+                regroup(x_t[r], r, X)
             if live(r - LAG_Y):
                 transpose_x1(r - LAG_Y)
                 regroup(x1_t[r - LAG_Y], r, X1)

@@ -25,6 +25,7 @@ QUADRANTS = 4
 LAG_M1 = 3
 LAG_Y = 4
 LAG_M2 = 6
+VECTOR_SHARE = 64
 HEAD_LOADS = PAIR * (LAG_M1 + 1) // LOAD_TILES
 X1 = 0
 X = 1
@@ -196,13 +197,24 @@ def tile_precomputedmetanet_pa_t_e_kernel(
         def finish_by_scalar_and_gpsimd(g, i):
             scaled = short.tile([P, D], F32)
             nc.scalar.activation(
-                out=scaled[:],
-                in_=products2[g][i][:],
+                out=scaled[:, VECTOR_SHARE:],
+                in_=products2[g][i][:, VECTOR_SHARE:],
                 func=COPY,
                 scale=coeff_f32[:, PAIR * g + i, 1:2],
             )
             nc.gpsimd.tensor_tensor(
-                out=results[g][:, i, :], in0=scaled[:], in1=x1_kept[g][:, i, :], op=ADD
+                out=results[g][:, i, VECTOR_SHARE:],
+                in0=scaled[:, VECTOR_SHARE:],
+                in1=x1_kept[g][:, i, VECTOR_SHARE:],
+                op=ADD,
+            )
+            nc.vector.scalar_tensor_tensor(
+                out=results[g][:, i, :VECTOR_SHARE],
+                in0=products2[g][i][:, :VECTOR_SHARE],
+                scalar=coeff_bf16[:, PAIR * g + i, 1:2],
+                in1=x1_kept[g][:, i, :VECTOR_SHARE],
+                op0=MULT,
+                op1=ADD,
             )
 
         def finish_by_vector(g, i):

@@ -25,7 +25,7 @@ QUADRANTS = 4
 LAG_M1 = 3
 LAG_Y = 4
 LAG_M2 = 6
-VECTOR_SHARE = 64
+VECTOR_SHARE = 96
 HEAD_LOADS = PAIR * (LAG_M1 + 1) // LOAD_TILES
 X1 = 0
 X = 1
@@ -87,7 +87,6 @@ def tile_precomputedmetanet_pa_t_e_kernel(
         for c in range(HEAD_LOADS, HEAD_LOADS + LOADS_AHEAD):
             load_x(c * LOAD_TILES, LOAD_TILES)
         coeff_f32 = keep.tile([P, TILES, STEPS], F32)
-        nc.gpsimd.tensor_copy(out=coeff_f32[:], in_=coeff_bf16[:])
 
         def live(g):
             return 0 <= g < PAIRS
@@ -190,7 +189,14 @@ def tile_precomputedmetanet_pa_t_e_kernel(
                     )
 
         def multiply2(g):
-            products2[g] = [banks1.tile([P, D], F32, name="product2_%d" % i) for i in range(PAIR)]
+            if g == PAIRS - 2:
+                products2[g] = [banks2.tile([P, D], F32, name="x_t") for i in range(PAIR)]
+            elif g == PAIRS - 1:
+                products2[g] = [banks2.tile([P, D], F32, name="product1") for i in range(PAIR)]
+            else:
+                products2[g] = [
+                    banks1.tile([P, D], F32, name="product2_%d" % i) for i in range(PAIR)
+                ]
             for i in range(PAIR):
                 multiply(products2[g][i], g + LAG_Y, X1, i, 1)
 
@@ -249,6 +255,8 @@ def tile_precomputedmetanet_pa_t_e_kernel(
                 c = r * PAIR // LOAD_TILES + HEAD_LOADS + LOADS_AHEAD
                 if c < TILES // LOAD_TILES:
                     load_x(c * LOAD_TILES, LOAD_TILES)
+            if r == LAG_M1 + 1:
+                nc.vector.tensor_copy(out=coeff_f32[:], in_=coeff_bf16[:])
             if live(r - LAG_M1):
                 multiply1(r - LAG_M1)
                 add1(r - LAG_M1, 0)

@@ -26,6 +26,7 @@ LAG_M1 = 3
 LAG_Y = 4
 LAG_M2 = 6
 VECTOR_SHARE = 96
+GPSIMD_WORDS = 96
 HEAD_LOADS = PAIR * (LAG_M1 + 1) // LOAD_TILES
 X1 = 0
 X = 1
@@ -166,14 +167,22 @@ def tile_precomputedmetanet_pa_t_e_kernel(
             if i == 0:
                 x1_rounded[g] = short.tile([P, PAIR, 2, P, 2], BF16, name="x1_rounded")
                 nc.gpsimd.tensor_scalar(
-                    out=x1_rounded[g][:, 0, :, :, :],
-                    in0=x1_kept[g][:, 0, :].rearrange("s (p u e) -> s u p e", u=2, e=2),
+                    out=x1_rounded[g][:, 0, :, :GPSIMD_WORDS, :],
+                    in0=x1_kept[g][:, 0, : PACK * GPSIMD_WORDS].rearrange(
+                        "s (p u e) -> s u p e", u=2, e=2
+                    ),
                     scalar1=1.0,
                     scalar2=0.0,
                     op0=MULT,
                     op1=ADD,
                 )
             else:
+                nc.scalar.copy(
+                    out=x1_rounded[g][:, 0, :, GPSIMD_WORDS:, :],
+                    in_=x1_kept[g][:, 0, PACK * GPSIMD_WORDS :].rearrange(
+                        "s (p u e) -> s u p e", u=2, e=2
+                    ),
+                )
                 nc.scalar.copy(
                     out=x1_rounded[g][:, 1, :, :, :],
                     in_=x1_kept[g][:, 1, :].rearrange("s (p u e) -> s u p e", u=2, e=2),

@@ -25,7 +25,7 @@ QUADRANTS = 4
 LAG_M1 = 3
 LAG_Y = 4
 LAG_M2 = 6
-VECTOR_SHARE = 96
+VECTOR_SHARE = 64
 GPSIMD_WORDS = 96
 HEAD_LOADS = PAIR * (LAG_M1 + 1) // LOAD_TILES
 X1 = 0

@@ -48,7 +48,7 @@ def tile_precomputedmetanet_pa_t_e_kernel(
     ) as quantised, tc.tile_pool(name="stored", bufs=6) as stored, tc.psum_pool(
         name="banks2", bufs=2
     ) as banks2, tc.psum_pool(name="banks1", bufs=1) as banks1, tc.manual_schedule():
-        w_scales = keep.tile([P, STEPS, D], U8, align_bytes=64)
+        w_scales = keep.tile([P, STEPS, D], U8, align_bytes=256)
         nc.vector.memset(w_scales[:].bitcast(I32), 0)
         identity = keep.tile([P, P], F32)
         make_identity(nc, identity[:])
@@ -63,7 +63,7 @@ def tile_precomputedmetanet_pa_t_e_kernel(
                 out=x_loads[c][:, at : at + count, :], in_=x_dram[:, first : first + count, :]
             )
 
-        w_words = keep.tile([P, STEPS, D], U32, align_bytes=64)
+        w_words = keep.tile([P, STEPS, D], U32, align_bytes=256)
 
         def load_words(step):
             nc.sync.dma_start(
@@ -122,8 +122,8 @@ def tile_precomputedmetanet_pa_t_e_kernel(
         def quantise(s):
             halves = [h for h in (X1, X) if live(s - LAG_Y if h == X1 else s)]
             first, count = halves[0], len(halves)
-            codes[s] = quantised.tile([P, 2, PAIR, P], U32, align_bytes=64, name="codes")
-            scales[s] = quantised.tile([P, 2, PAIR, P], U8, align_bytes=64, name="scales")
+            codes[s] = quantised.tile([P, 2, PAIR, P], U32, align_bytes=256, name="codes")
+            scales[s] = quantised.tile([P, 2, PAIR, P], U8, align_bytes=256, name="scales")
             nc.vector.quantize_mx(
                 out=codes[s][:, first : first + count, :, :]
                 .rearrange("p h i r -> p (h i r)")

@@ -25,7 +25,7 @@ QUADRANTS = 4
 LAG_M1 = 3
 LAG_Y = 4
 LAG_M2 = 6
-VECTOR_SHARE = 64
+VECTOR_SHARE = 80
 GPSIMD_WORDS = 96
 HEAD_LOADS = PAIR * (LAG_M1 + 1) // LOAD_TILES
 X1 = 0
@@ -163,30 +163,24 @@ def tile_precomputedmetanet_pa_t_e_kernel(
                 op1=ADD,
             )
 
-        def round_x1(g, i):
-            if i == 0:
-                x1_rounded[g] = short.tile([P, PAIR, 2, P, 2], BF16, name="x1_rounded")
-                nc.gpsimd.tensor_scalar(
-                    out=x1_rounded[g][:, 0, :, :GPSIMD_WORDS, :],
-                    in0=x1_kept[g][:, 0, : PACK * GPSIMD_WORDS].rearrange(
-                        "s (p u e) -> s u p e", u=2, e=2
-                    ),
-                    scalar1=1.0,
-                    scalar2=0.0,
-                    op0=MULT,
-                    op1=ADD,
-                )
-            else:
-                nc.scalar.copy(
-                    out=x1_rounded[g][:, 0, :, GPSIMD_WORDS:, :],
-                    in_=x1_kept[g][:, 0, PACK * GPSIMD_WORDS :].rearrange(
-                        "s (p u e) -> s u p e", u=2, e=2
-                    ),
-                )
-                nc.scalar.copy(
-                    out=x1_rounded[g][:, 1, :, :, :],
-                    in_=x1_kept[g][:, 1, :].rearrange("s (p u e) -> s u p e", u=2, e=2),
-                )
+        def round_by_gpsimd(g):
+            x1_rounded[g] = short.tile([P, PAIR, 2, P, 2], BF16, name="x1_rounded")
+            nc.gpsimd.tensor_scalar(
+                out=x1_rounded[g][:, 1, :, :GPSIMD_WORDS, :],
+                in0=x1_kept[g][:, 1, : PACK * GPSIMD_WORDS].rearrange(
+                    "s (p u e) -> s u p e", u=2, e=2
+                ),
+                scalar1=1.0,
+                scalar2=0.0,
+                op0=MULT,
+                op1=ADD,
+            )
+
+        def round_by_scalar(g, i, first):
+            nc.scalar.copy(
+                out=x1_rounded[g][:, i, :, first:, :],
+                in_=x1_kept[g][:, i, PACK * first :].rearrange("s (p u e) -> s u p e", u=2, e=2),
+            )
 
         def transpose_x1(g):
             x1_t[g] = banks2.tile([P, PAIR, 2, P], F32, name="x1_t")
@@ -269,14 +263,16 @@ def tile_precomputedmetanet_pa_t_e_kernel(
             if live(r - LAG_M1):
                 multiply1(r - LAG_M1)
                 add1(r - LAG_M1, 0)
+                add1(r - LAG_M1, 1)
             if live(r - 1 - LAG_Y) or live(r - 1):
                 quantise(r - 1)
             if live(r - LAG_M1):
-                add1(r - LAG_M1, 1)
-                round_x1(r - LAG_M1, 0)
+                round_by_gpsimd(r - LAG_M1)
             if live(r - LAG_M2):
                 multiply2(r - LAG_M2)
                 finish(r - LAG_M2)
+            if live(r - LAG_M1):
+                round_by_scalar(r - LAG_M1, 0, 0)
             if live(r):
                 transpose_x(r)
                 regroup(x_t[r], r, X)
@@ -284,4 +280,4 @@ def tile_precomputedmetanet_pa_t_e_kernel(
                 transpose_x1(r - LAG_Y)
                 regroup(x1_t[r - LAG_Y], r, X1)
             if live(r - LAG_M1):
-                round_x1(r - LAG_M1, 1)
+                round_by_scalar(r - LAG_M1, 1, GPSIMD_WORDS)

@@ -28,6 +28,8 @@ LAG_M2 = 6
 VECTOR_SHARE = 80
 GPSIMD_WORDS = 96
 HEAD_LOADS = PAIR * (LAG_M1 + 1) // LOAD_TILES
+VECTOR_ROUNDS = 2
+DRAIN = PAIRS + LAG_M1 - LAG_M2
 X1 = 0
 X = 1
 
@@ -71,7 +73,9 @@ def tile_precomputedmetanet_pa_t_e_kernel(
                 in_=task_mats_words[step].rearrange("p n t -> p (n t)").bitcast(I32),
             )
 
-        for g in range(LAG_M1):
+        for i in range(PAIR):
+            load_x(i, 1)
+        for g in range(1, LAG_M1):
             load_x(PAIR * g, PAIR)
         for quadrant in range(QUADRANTS):
             nc.sync.dma_start(
@@ -114,7 +118,8 @@ def tile_precomputedmetanet_pa_t_e_kernel(
                     nc.tensor.transpose(x_t[g][:, i, u, :], words[:, u : D // 2 : 2], identity[:])
 
         def regroup(transposed, s, half):
-            nc.scalar.copy(
+            copy = nc.vector.tensor_copy if s < VECTOR_ROUNDS else nc.scalar.copy
+            copy(
                 out=grouped_of(s)[:, half, :, :, :].bitcast(F32),
                 in_=transposed[:].rearrange("p i u r -> p i r u"),
             )
@@ -157,7 +162,7 @@ def tile_precomputedmetanet_pa_t_e_kernel(
             nc.vector.scalar_tensor_tensor(
                 out=x1_kept[g][:, i, :],
                 in0=products1[g][i][:],
-                scalar=coeff_bf16[:, j, 0:1],
+                scalar=coeff_f32[:, j, 0:1],
                 in1=x_tile(j),
                 op0=MULT,
                 op1=ADD,
@@ -183,7 +188,7 @@ def tile_precomputedmetanet_pa_t_e_kernel(
             )
 
         def transpose_x1(g):
-            x1_t[g] = banks2.tile([P, PAIR, 2, P], F32, name="x1_t")
+            x1_t[g] = banks1.tile([P, PAIR, 2, P], F32, name="x1_t")
             for i in range(PAIR):
                 words = x1_rounded[g][:, i, :, :, :].rearrange("s u p e -> s (u p e)").bitcast(F32)
                 for u in range(2):
@@ -198,7 +203,8 @@ def tile_precomputedmetanet_pa_t_e_kernel(
                 products2[g] = [banks2.tile([P, D], F32, name="product1") for i in range(PAIR)]
             else:
                 products2[g] = [
-                    banks1.tile([P, D], F32, name="product2_%d" % i) for i in range(PAIR)
+                    banks1.tile([P, D], F32, name="product2_0"),
+                    banks2.tile([P, D], F32, name="product2_1"),
                 ]
             for i in range(PAIR):
                 multiply(products2[g][i], g + LAG_Y, X1, i, 1)
@@ -220,7 +226,7 @@ def tile_precomputedmetanet_pa_t_e_kernel(
             nc.vector.scalar_tensor_tensor(
                 out=results[g][:, i, :VECTOR_SHARE],
                 in0=products2[g][i][:, :VECTOR_SHARE],
-                scalar=coeff_bf16[:, PAIR * g + i, 1:2],
+                scalar=coeff_f32[:, PAIR * g + i, 1:2],
                 in1=x1_kept[g][:, i, :VECTOR_SHARE],
                 op0=MULT,
                 op1=ADD,
@@ -230,7 +236,7 @@ def tile_precomputedmetanet_pa_t_e_kernel(
             nc.vector.scalar_tensor_tensor(
                 out=results[g][:, i, :],
                 in0=products2[g][i][:],
-                scalar=coeff_bf16[:, PAIR * g + i, 1:2],
+                scalar=coeff_f32[:, PAIR * g + i, 1:2],
                 in1=x1_kept[g][:, i, :],
                 op0=MULT,
                 op1=ADD,
@@ -247,9 +253,12 @@ def tile_precomputedmetanet_pa_t_e_kernel(
             if g + LAG_M2 < PAIRS + LAG_M1:
                 finish_by_scalar_and_gpsimd(g, 0)
                 finish_by_vector(g, 1)
-                store(g, 0, PAIR)
+                store(g, 1, 1)
+                store(g, 0, 1)
             else:
                 for i in range(PAIR):
+                    if i == 1 and g == DRAIN:
+                        quantise(g + LAG_M2 - 1)
                     finish_by_vector(g, i)
                     store(g, i, 1)
 
@@ -258,13 +267,13 @@ def tile_precomputedmetanet_pa_t_e_kernel(
                 c = r * PAIR // LOAD_TILES + HEAD_LOADS + LOADS_AHEAD
                 if c < TILES // LOAD_TILES:
                     load_x(c * LOAD_TILES, LOAD_TILES)
-            if r == LAG_M1 + 1:
+            if r == LAG_M1:
                 nc.vector.tensor_copy(out=coeff_f32[:], in_=coeff_bf16[:])
             if live(r - LAG_M1):
                 multiply1(r - LAG_M1)
                 add1(r - LAG_M1, 0)
                 add1(r - LAG_M1, 1)
-            if live(r - 1 - LAG_Y) or live(r - 1):
+            if (live(r - 1 - LAG_Y) or live(r - 1)) and r - LAG_M2 != DRAIN:
                 quantise(r - 1)
             if live(r - LAG_M1):
                 round_by_gpsimd(r - LAG_M1)

import concourse.mybir as mybir
from concourse.masks import make_identity

F32 = mybir.dt.float32
BF16 = mybir.dt.bfloat16
I32 = mybir.dt.int32
U32 = mybir.dt.uint32
U8 = mybir.dt.uint8
FP8X4 = mybir.dt.float8_e4m3fn_x4
MULT = mybir.AluOpType.mult
ADD = mybir.AluOpType.add
COPY = mybir.ActivationFunctionType.Copy

P = 128
PACK = 4
SAMPLES = 8192
D = 512
STEPS = 2
TILES = SAMPLES // P
PAIR = 2
PAIRS = TILES // PAIR
LOAD_TILES = 4
LOADS_AHEAD = 2
QUADRANTS = 4
LAG_M1 = 3
LAG_Y = 4
LAG_M2 = 6
VECTOR_SHARE = 80
GPSIMD_WORDS = 96
HEAD_LOADS = PAIR * (LAG_M1 + 1) // LOAD_TILES
VECTOR_ROUNDS = 2
DRAIN = PAIRS + LAG_M1 - LAG_M2
X1 = 0
X = 1

FLOPS = 2 * STEPS * SAMPLES * D * D


def tile_precomputedmetanet_pa_t_e_kernel(
    tc, transformed, coeff, task_mats_words, task_mats_scales, out
):
    nc = tc.nc
    x_dram = transformed.rearrange("(p j) d -> p j d", j=TILES)
    out_dram = out.rearrange("(p j) d -> p j d", j=TILES)

    with tc.tile_pool(name="keep", bufs=1) as keep, tc.tile_pool(
        name="short", bufs=3
    ) as short, tc.tile_pool(name="long", bufs=6) as long_lived, tc.tile_pool(
        name="quantised", bufs=4
    ) as quantised, tc.tile_pool(name="stored", bufs=6) as stored, tc.psum_pool(
        name="banks2", bufs=2
    ) as banks2, tc.psum_pool(name="banks1", bufs=1) as banks1, tc.manual_schedule():
        w_scales = keep.tile([P, STEPS, D], U8, align_bytes=256)
        nc.vector.memset(w_scales[:].bitcast(I32), 0)
        identity = keep.tile([P, P], F32)
        make_identity(nc, identity[:])

        x_loads = []
        for c in range(TILES // LOAD_TILES):
            x_loads.append(keep.tile([P, LOAD_TILES, D], BF16, name="x_load%d" % c))

        def load_x(first, count):
            c, at = first // LOAD_TILES, first % LOAD_TILES
            nc.sync.dma_start(
                out=x_loads[c][:, at : at + count, :], in_=x_dram[:, first : first + count, :]
            )

        w_words = keep.tile([P, STEPS, D], U32, align_bytes=256)

        def load_words(step):
            nc.sync.dma_start(
                out=w_words[:, step, :].bitcast(I32),
                in_=task_mats_words[step].rearrange("p n t -> p (n t)").bitcast(I32),
            )

        for i in range(PAIR):
            load_x(i, 1)
        for g in range(1, LAG_M1):
            load_x(PAIR * g, PAIR)
        for quadrant in range(QUADRANTS):
            nc.sync.dma_start(
                out=w_scales[32 * quadrant : 32 * quadrant + 4, :, :].bitcast(I32),
                in_=task_mats_scales[:, 4 * quadrant : 4 * quadrant + 4, :]
                .bitcast(I32)
                .rearrange("s r n -> r s n"),
            )
        load_words(0)
        coeff_bf16 = keep.tile([P, TILES, STEPS], BF16)
        nc.sync.dma_start(out=coeff_bf16[:], in_=coeff.rearrange("(p j) s -> p j s", j=TILES))
        load_x(PAIR * LAG_M1, PAIR)
        load_words(1)
        for c in range(HEAD_LOADS, HEAD_LOADS + LOADS_AHEAD):
            load_x(c * LOAD_TILES, LOAD_TILES)
        coeff_f32 = keep.tile([P, TILES, STEPS], F32)

        def live(g):
            return 0 <= g < PAIRS

        def x_tile(j):
            return x_loads[j // LOAD_TILES][:, j % LOAD_TILES, :]

        x_t, products1, x1_kept, x1_rounded = {}, {}, {}, {}
        x1_t, products2, results = {}, {}, {}
        grouped, codes, scales = {}, {}, {}

        def grouped_of(s):
            if s not in grouped:
                grouped[s] = short.tile(
                    [P, 2, PAIR, P, PACK], BF16, align_bytes=64, name="grouped"
                )
            return grouped[s]

        def transpose_x(g):
            x_t[g] = banks2.tile([P, PAIR, 2, P], F32, name="x_t")
            for i in range(PAIR):
                words = x_tile(PAIR * g + i).bitcast(F32)
                for u in range(2):
                    nc.tensor.transpose(x_t[g][:, i, u, :], words[:, u : D // 2 : 2], identity[:])

        def regroup(transposed, s, half):
            copy = nc.vector.tensor_copy if s < VECTOR_ROUNDS else nc.scalar.copy
            copy(
                out=grouped_of(s)[:, half, :, :, :].bitcast(F32),
                in_=transposed[:].rearrange("p i u r -> p i r u"),
            )

        def quantise(s):
            halves = [h for h in (X1, X) if live(s - LAG_Y if h == X1 else s)]
            first, count = halves[0], len(halves)
            codes[s] = quantised.tile([P, 2, PAIR, P], U32, align_bytes=256, name="codes")
            scales[s] = quantised.tile([P, 2, PAIR, P], U8, align_bytes=256, name="scales")
            nc.vector.quantize_mx(
                out=codes[s][:, first : first + count, :, :]
                .rearrange("p h i r -> p (h i r)")
                .bitcast(FP8X4),
                scales=scales[s][:, first : first + count, :, :].rearrange("p h i r -> p (h i r)"),
                in_=grouped[s][:, first : first + count, :, :, :].rearrange(
                    "p h i r t -> p (h i r t)"
                ),
            )

        def multiply(product, s, half, i, step):
            nc.tensor.matmul_mx(
                out=product[:],
                lhsT=codes[s][:, half, i, :].bitcast(FP8X4),
                lhsT_scale=scales[s][:, half, i, :],
                rhs=w_words[:, step, :].bitcast(FP8X4),
                rhs_scale=w_scales[:, step, :],
                start=True,
                stop=True,
            )

        def multiply1(g):
            products1[g] = [banks2.tile([P, D], F32, name="product1") for i in range(PAIR)]
            for i in range(PAIR):
                multiply(products1[g][i], g, X, i, 0)

        def add1(g, i):
            if i == 0:
                x1_kept[g] = long_lived.tile([P, PAIR, D], F32, name="x1_kept")
            j = PAIR * g + i
            nc.vector.scalar_tensor_tensor(
                out=x1_kept[g][:, i, :],
                in0=products1[g][i][:],
                scalar=coeff_f32[:, j, 0:1],
                in1=x_tile(j),
                op0=MULT,
                op1=ADD,
            )

        def round_by_gpsimd(g):
            x1_rounded[g] = short.tile([P, PAIR, 2, P, 2], BF16, name="x1_rounded")
            nc.gpsimd.tensor_scalar(
                out=x1_rounded[g][:, 1, :, :GPSIMD_WORDS, :],
                in0=x1_kept[g][:, 1, : PACK * GPSIMD_WORDS].rearrange(
                    "s (p u e) -> s u p e", u=2, e=2
                ),
                scalar1=1.0,
                scalar2=0.0,
                op0=MULT,
                op1=ADD,
            )

        def round_by_scalar(g, i, first):
            nc.scalar.copy(
                out=x1_rounded[g][:, i, :, first:, :],
                in_=x1_kept[g][:, i, PACK * first :].rearrange("s (p u e) -> s u p e", u=2, e=2),
            )

        def transpose_x1(g):
            x1_t[g] = banks1.tile([P, PAIR, 2, P], F32, name="x1_t")
            for i in range(PAIR):
                words = x1_rounded[g][:, i, :, :, :].rearrange("s u p e -> s (u p e)").bitcast(F32)
                for u in range(2):
                    nc.tensor.transpose(
                        x1_t[g][:, i, u, :], words[:, u * P : (u + 1) * P], identity[:]
                    )

        def multiply2(g):
            if g == PAIRS - 2:
                products2[g] = [banks2.tile([P, D], F32, name="x_t") for i in range(PAIR)]
            elif g == PAIRS - 1:
                products2[g] = [banks2.tile([P, D], F32, name="product1") for i in range(PAIR)]
            else:
                products2[g] = [
                    banks1.tile([P, D], F32, name="product2_0"),
                    banks2.tile([P, D], F32, name="product2_1"),
                ]
            for i in range(PAIR):
                multiply(products2[g][i], g + LAG_Y, X1, i, 1)

        def finish_by_scalar_and_gpsimd(g, i):
            scaled = short.tile([P, D], F32)
            nc.scalar.activation(
                out=scaled[:, VECTOR_SHARE:],
                in_=products2[g][i][:, VECTOR_SHARE:],
                func=COPY,
                scale=coeff_f32[:, PAIR * g + i, 1:2],
            )
            nc.gpsimd.tensor_tensor(
                out=results[g][:, i, VECTOR_SHARE:],
                in0=scaled[:, VECTOR_SHARE:],
                in1=x1_kept[g][:, i, VECTOR_SHARE:],
                op=ADD,
            )
            nc.vector.scalar_tensor_tensor(
                out=results[g][:, i, :VECTOR_SHARE],
                in0=products2[g][i][:, :VECTOR_SHARE],
                scalar=coeff_f32[:, PAIR * g + i, 1:2],
                in1=x1_kept[g][:, i, :VECTOR_SHARE],
                op0=MULT,
                op1=ADD,
            )

        def finish_by_vector(g, i):
            nc.vector.scalar_tensor_tensor(
                out=results[g][:, i, :],
                in0=products2[g][i][:],
                scalar=coeff_f32[:, PAIR * g + i, 1:2],
                in1=x1_kept[g][:, i, :],
                op0=MULT,
                op1=ADD,
            )

        def store(g, first, count):
            j = PAIR * g + first
            nc.sync.dma_start(
                out=out_dram[:, j : j + count, :], in_=results[g][:, first : first + count, :]
            )

        def finish(g):
            results[g] = stored.tile([P, PAIR, D], F32, name="result")
            if g + LAG_M2 < PAIRS + LAG_M1:
                finish_by_scalar_and_gpsimd(g, 0)
                finish_by_vector(g, 1)
                store(g, 1, 1)
                store(g, 0, 1)
            else:
                for i in range(PAIR):
                    if i == 1 and g == DRAIN:
                        quantise(g + LAG_M2 - 1)
                    finish_by_vector(g, i)
                    store(g, i, 1)

        for r in range(PAIRS + LAG_M2):
            if r % (LOAD_TILES // PAIR) == 0:
                c = r * PAIR // LOAD_TILES + HEAD_LOADS + LOADS_AHEAD
                if c < TILES // LOAD_TILES:
                    load_x(c * LOAD_TILES, LOAD_TILES)
            if r == LAG_M1:
                nc.vector.tensor_copy(out=coeff_f32[:], in_=coeff_bf16[:])
            if live(r - LAG_M1):
                multiply1(r - LAG_M1)
                add1(r - LAG_M1, 0)
                add1(r - LAG_M1, 1)
            if (live(r - 1 - LAG_Y) or live(r - 1)) and r - LAG_M2 != DRAIN:
                quantise(r - 1)
            if live(r - LAG_M1):
                round_by_gpsimd(r - LAG_M1)
            if live(r - LAG_M2):
                multiply2(r - LAG_M2)
                finish(r - LAG_M2)
            if live(r - LAG_M1):
                round_by_scalar(r - LAG_M1, 0, 0)
            if live(r):
                transpose_x(r)
                regroup(x_t[r], r, X)
            if live(r - LAG_Y):
                transpose_x1(r - LAG_Y)
                regroup(x1_t[r - LAG_Y], r, X1)
            if live(r - LAG_M1):
                round_by_scalar(r - LAG_M1, 1, GPSIMD_WORDS)
